import numpy as np
import ml_dtypes


def mxq(x, axis, fmt="e4m3"):
    dtype, down = {"e4m3": (ml_dtypes.float8_e4m3fn, 7), "e5m2": (ml_dtypes.float8_e5m2, 14)}[fmt]
    v = np.moveaxis(np.asarray(x, np.float32).astype(ml_dtypes.bfloat16).astype(np.float64), axis, -1)
    blocks = v.reshape(v.shape[:-1] + (-1, 32))
    amax = np.abs(blocks).max(-1, keepdims=True)
    byte = np.maximum(np.where(amax > 0, np.frexp(amax)[1] - 1 + 127, 0) - down, 1)
    scale = np.exp2(byte - 127.0)
    codes = (blocks / scale).astype(np.float32).astype(dtype).astype(np.float64)
    return np.moveaxis((codes * scale).reshape(v.shape), -1, axis)


WIDE = False


def mx_kscale(k):
    if not WIDE:
        return np.ones(k)
    levels = np.array([20, -20, 10, -10, 0])
    a = np.random.permutation(np.resize(levels, k // 512 * 4)).reshape(k // 512, 4)
    idx = np.arange(k)
    return np.exp2(a[idx // 512, idx % 128 // 32])


BF16 = ml_dtypes.bfloat16


def bf(x):
    return np.asarray(x, np.float32).astype(BF16)


def f64(x):
    return np.asarray(x).astype(np.float64)


B, S, IN_F, OUT_F, GROUP_SIZE = 4, 1024, 1024, 512, 128


def make_weight(sign_weights, scales):
    binary = np.sign(f64(sign_weights))
    scale_mat = np.repeat(f64(scales), GROUP_SIZE).reshape(OUT_F, IN_F)
    return binary * scale_mat


def setup_inputs():
    u = mx_kscale(OUT_F)
    x = np.random.standard_normal((B, S, IN_F))
    sw = np.random.standard_normal((OUT_F, IN_F))
    sw = np.where(sw == 0, 1.0, sw)
    scales = np.random.uniform(0.32, 3.2, OUT_F * IN_F // GROUP_SIZE) / np.sqrt(IN_F) / np.repeat(u, IN_F // GROUP_SIZE)
    g = np.random.standard_normal((B, S, OUT_F)) * np.exp2(np.random.randint(-12, 1, (B, S, 1))) * 4.0 * u
    return {"x": bf(x), "sign_weights": bf(sw), "scales": bf(scales), "grad_out": bf(g)}


def reference(x, sign_weights, scales, grad_out):
    weight = make_weight(sign_weights, scales)
    return mxq(f64(grad_out), 2, "e5m2") @ mxq(weight, 0, "e4m3")

@@ -1,0 +1,170 @@
+from contextlib import ExitStack
+
+import concourse.mybir as mybir
+from concourse.masks import make_identity
+
+F32 = mybir.dt.float32
+BF16 = mybir.dt.bfloat16
+U32 = mybir.dt.uint32
+U8 = mybir.dt.uint8
+E4M3X4 = mybir.dt.float8_e4m3fn_x4
+E5M2X4 = mybir.dt.float8_e5m2_x4
+ACT = mybir.ActivationFunctionType
+ALU = mybir.AluOpType
+
+P = 128
+TOKENS = 4096
+OUT_F = 512
+IN_F = 1024
+GROUPS = 8
+NT = TOKENS // P
+HALF = 512
+
+FLOPS = 2 * TOKENS * OUT_F * IN_F
+BYTES = TOKENS * OUT_F * 2 + OUT_F * IN_F * 2 + OUT_F * GROUPS * 2 + TOKENS * IN_F * 4
+
+MANUAL = False
+LOAD_CHUNKS = [4, 4, 8, 8, 8]
+STORE_GROUPS = [1, 1, 2, 4, 4, 4, 4, 4, 4, 4]
+QG = 4
+
+
+def tile_stebitlinear_t_kernel(tc, x, sign_weights, scales, grad_out, out):
+    nc = tc.nc
+    g_view = grad_out.flatten_outer_dims().rearrange("(p r) o -> p r o", r=NT)
+    out_view = out.flatten_outer_dims().rearrange("(p r) i -> p r i", r=NT)
+
+    with ExitStack() as ctx:
+        if MANUAL:
+            ctx.enter_context(tc.manual_schedule())
+        keep = ctx.enter_context(tc.tile_pool(name="keep", bufs=1))
+        stage = ctx.enter_context(tc.tile_pool(name="stage", bufs=3))
+        psum_t = ctx.enter_context(tc.psum_pool(name="psum_t", bufs=2))
+        psum_o = ctx.enter_context(tc.psum_pool(name="psum_o", bufs=6))
+
+        sc_raw = keep.tile([P, 4, GROUPS], BF16, name="sc_raw")
+        nc.scalar.dma_start(
+            out=sc_raw[:].rearrange("p (u e) g -> p u (e g)", u=2),
+            in_=scales.rearrange("(u q s) -> q u s", u=2, s=2 * GROUPS),
+        )
+        w_raw = keep.tile([P, 4, IN_F], BF16, name="w_raw")
+        for u in range(2):
+            nc.sync.dma_start(
+                out=w_raw[:, 2 * u : 2 * u + 2, :],
+                in_=sign_weights[256 * u : 256 * u + 256, :].rearrange("(q e) c -> q e c", e=2),
+            )
+        g_tiles = []
+        r0 = 0
+        for ci, n in enumerate(LOAD_CHUNKS):
+            g_sb = keep.tile([P, n * OUT_F], BF16, name="g_sb%d" % ci)
+            nc.sync.dma_start(
+                out=g_sb[:].rearrange("p (r o) -> p r o", r=n), in_=g_view[:, r0 : r0 + n, :]
+            )
+            for k in range(n):
+                g_tiles.append((g_sb, k))
+            r0 += n
+
+        ident = keep.tile([P, P], F32, name="ident")
+        make_identity(nc, ident[:])
+
+        warm = keep.tile([P, 1], F32, name="warm")
+        warm2 = keep.tile([P, 1], F32, name="warm2")
+        nc.vector.memset(warm[:], 0.0)
+        nc.scalar.activation(out=warm2[:], in_=warm[:], func=ACT.Sign)
+
+        sc_gt = keep.tile([P, GROUPS, 4], BF16, name="sc_gt")
+        nc.vector.tensor_copy(out=sc_gt[:], in_=sc_raw[:].rearrange("p t g -> p g t"))
+        sgn = keep.tile([P, IN_F * 4], BF16, name="sgn")
+        w_grp = keep.tile([P, IN_F * 4], BF16, name="w_grp", align_bytes=64)
+        w_codes = keep.tile([P, IN_F], U32, name="w_codes", align_bytes=64)
+        w_scales = keep.tile([P, IN_F], U8, name="w_scales", align_bytes=64)
+        PC = 256
+        for pc in range(IN_F // PC):
+            c0 = pc * PC
+            nc.scalar.activation(
+                out=sgn[:, 4 * c0 : 4 * (c0 + PC)].rearrange("p (c i t) -> p c t i", i=4, t=4),
+                in_=w_raw[:, :, c0 : c0 + PC].rearrange("p t (c i) -> p c t i", i=4),
+                func=ACT.Sign,
+            )
+        for pc in range(IN_F // PC):
+            c0 = pc * PC
+            ng = PC // 128
+            nc.vector.tensor_tensor(
+                out=w_grp[:, 4 * c0 : 4 * (c0 + PC)].rearrange("p (g c t) -> p g c t", g=ng, t=4),
+                in0=sgn[:, 4 * c0 : 4 * (c0 + PC)].rearrange("p (g c t) -> p g c t", g=ng, t=4),
+                in1=sc_gt[:, pc * ng : (pc + 1) * ng, :].unsqueeze(2).to_broadcast([P, ng, 128, 4]),
+                op=ALU.mult,
+            )
+            if pc % 2 == 1:
+                h = pc // 2
+                nc.vector.quantize_mx(
+                    out=w_codes[:, h * HALF : (h + 1) * HALF].bitcast(E4M3X4),
+                    scales=w_scales[:, h * HALF : (h + 1) * HALF],
+                    in_=w_grp[:, 4 * h * HALF : 4 * (h + 1) * HALF],
+                )
+
+        g_codes = keep.tile([P, TOKENS], U32, name="g_codes", align_bytes=64)
+        g_scales = keep.tile([P, TOKENS], U8, name="g_scales", align_bytes=64)
+
+        def prepare(j):
+            grouped = stage.tile([P, QG * 512], BF16, name="grouped", align_bytes=64)
+            gr32 = grouped[:].bitcast(F32).rearrange("p (r m u) -> p r m u", r=QG, u=2)
+            for b in range(QG // 2):
+                xt = psum_t.tile([P, 4, P], F32, name="xt")
+                for rr in range(2):
+                    g_sb, k = g_tiles[j * QG + 2 * b + rr]
+                    words = g_sb[:].bitcast(F32)
+                    for u in range(2):
+                        nc.tensor.transpose(
+                            xt[:, 2 * rr + u, :],
+                            words[:, k * 256 + 128 * u : k * 256 + 128 * u + 128],
+                            ident[:],
+                        )
+                nc.scalar.copy(
+                    out=gr32[:, 2 * b : 2 * b + 2, :, :],
+                    in_=xt[:].rearrange("p (r u) m -> p r m u", u=2),
+                )
+            nc.vector.quantize_mx(
+                out=g_codes[:, j * QG * P : (j + 1) * QG * P].bitcast(E5M2X4),
+                scales=g_scales[:, j * QG * P : (j + 1) * QG * P],
+                in_=grouped[:],
+            )
+
+        store_of = {}
+        r0 = 0
+        for si, n in enumerate(STORE_GROUPS):
+            for k in range(n):
+                store_of[r0 + k] = (si, k, n, r0)
+            r0 += n
+        o_tiles = {}
+
+        def multiply(r):
+            si, k, n, first = store_of[r]
+            if k == 0:
+                o_tiles[si] = keep.tile([P, n, IN_F], F32, name="o_sb%d" % si)
+            o_sb = o_tiles[si]
+            for h in range(2):
+                acc = psum_o.tile([P, HALF], F32, name="acc")
+                nc.tensor.matmul_mx(
+                    out=acc[:],
+                    lhsT=g_codes[:, r * P : (r + 1) * P].bitcast(E5M2X4),
+                    lhsT_scale=g_scales[:, r * P : (r + 1) * P],
+                    rhs=w_codes[:, h * HALF : (h + 1) * HALF].bitcast(E4M3X4),
+                    rhs_scale=w_scales[:, h * HALF : (h + 1) * HALF],
+                    start=True,
+                    stop=True,
+                )
+                if h == 0:
+                    nc.vector.tensor_copy(out=o_sb[:, k, 0:HALF], in_=acc[:])
+                else:
+                    nc.scalar.copy(out=o_sb[:, k, HALF:IN_F], in_=acc[:])
+            if k == n - 1:
+                nc.sync.dma_start(out=out_view[:, first : first + n, :], in_=o_sb[:])
+
+        n_q = NT // QG
+        prepare(0)
+        for j in range(n_q):
+            if j + 1 < n_q:
+                prepare(j + 1)
+            for r in range(j * QG, (j + 1) * QG):
+                multiply(r)

@@ -23,10 +23,12 @@ HALF = 512
 FLOPS = 2 * TOKENS * OUT_F * IN_F
 BYTES = TOKENS * OUT_F * 2 + OUT_F * IN_F * 2 + OUT_F * GROUPS * 2 + TOKENS * IN_F * 4
 
-MANUAL = False
+MANUAL = True
 LOAD_CHUNKS = [4, 4, 8, 8, 8]
-STORE_GROUPS = [1, 1, 2, 4, 4, 4, 4, 4, 4, 4]
-QG = 4
+STORE_GROUPS = [1, 1, 1, 1, 1, 1, 1, 1, 2, 2, 2, 4, 4, 4, 4]
+LEAD = 2
+PC = 256
+NB = NT // 2
 
 
 def tile_stebitlinear_t_kernel(tc, x, sign_weights, scales, grad_out, out):
@@ -38,7 +40,7 @@ def tile_stebitlinear_t_kernel(tc, x, sign_weights, scales, grad_out, out):
         if MANUAL:
             ctx.enter_context(tc.manual_schedule())
         keep = ctx.enter_context(tc.tile_pool(name="keep", bufs=1))
-        stage = ctx.enter_context(tc.tile_pool(name="stage", bufs=3))
+        stage = ctx.enter_context(tc.tile_pool(name="stage", bufs=4))
         psum_t = ctx.enter_context(tc.psum_pool(name="psum_t", bufs=2))
         psum_o = ctx.enter_context(tc.psum_pool(name="psum_o", bufs=6))
 
@@ -78,15 +80,32 @@ def tile_stebitlinear_t_kernel(tc, x, sign_weights, scales, grad_out, out):
         w_grp = keep.tile([P, IN_F * 4], BF16, name="w_grp", align_bytes=64)
         w_codes = keep.tile([P, IN_F], U32, name="w_codes", align_bytes=64)
         w_scales = keep.tile([P, IN_F], U8, name="w_scales", align_bytes=64)
-        PC = 256
-        for pc in range(IN_F // PC):
+        g_codes = keep.tile([P, TOKENS], U32, name="g_codes", align_bytes=64)
+        g_scales = keep.tile([P, TOKENS], U8, name="g_scales", align_bytes=64)
+
+        def sign(pc):
             c0 = pc * PC
             nc.scalar.activation(
                 out=sgn[:, 4 * c0 : 4 * (c0 + PC)].rearrange("p (c i t) -> p c t i", i=4, t=4),
                 in_=w_raw[:, :, c0 : c0 + PC].rearrange("p t (c i) -> p c t i", i=4),
                 func=ACT.Sign,
             )
-        for pc in range(IN_F // PC):
+
+        def sign_on_vector(pc):
+            c0 = pc * PC
+            tiny = 2.0 ** -69
+            clipped = keep.tile([P, 4, PC], BF16, name="clipped")
+            nc.vector.tensor_scalar(
+                out=clipped[:], in0=w_raw[:, :, c0 : c0 + PC],
+                scalar1=2.0 ** 64, scalar2=tiny, op0=ALU.mult, op1=ALU.min,
+            )
+            nc.vector.tensor_scalar(
+                out=sgn[:, 4 * c0 : 4 * (c0 + PC)].rearrange("p (c i t) -> p c t i", i=4, t=4),
+                in0=clipped[:].rearrange("p t (c i) -> p c t i", i=4),
+                scalar1=-tiny, scalar2=2.0 ** 69, op0=ALU.max, op1=ALU.mult,
+            )
+
+        def mul(pc):
             c0 = pc * PC
             ng = PC // 128
             nc.vector.tensor_tensor(
@@ -95,76 +114,129 @@ def tile_stebitlinear_t_kernel(tc, x, sign_weights, scales, grad_out, out):
                 in1=sc_gt[:, pc * ng : (pc + 1) * ng, :].unsqueeze(2).to_broadcast([P, ng, 128, 4]),
                 op=ALU.mult,
             )
-            if pc % 2 == 1:
-                h = pc // 2
-                nc.vector.quantize_mx(
-                    out=w_codes[:, h * HALF : (h + 1) * HALF].bitcast(E4M3X4),
-                    scales=w_scales[:, h * HALF : (h + 1) * HALF],
-                    in_=w_grp[:, 4 * h * HALF : 4 * (h + 1) * HALF],
-                )
 
-        g_codes = keep.tile([P, TOKENS], U32, name="g_codes", align_bytes=64)
-        g_scales = keep.tile([P, TOKENS], U8, name="g_scales", align_bytes=64)
-
-        def prepare(j):
-            grouped = stage.tile([P, QG * 512], BF16, name="grouped", align_bytes=64)
-            gr32 = grouped[:].bitcast(F32).rearrange("p (r m u) -> p r m u", r=QG, u=2)
-            for b in range(QG // 2):
-                xt = psum_t.tile([P, 4, P], F32, name="xt")
-                for rr in range(2):
-                    g_sb, k = g_tiles[j * QG + 2 * b + rr]
-                    words = g_sb[:].bitcast(F32)
-                    for u in range(2):
-                        nc.tensor.transpose(
-                            xt[:, 2 * rr + u, :],
-                            words[:, k * 256 + 128 * u : k * 256 + 128 * u + 128],
-                            ident[:],
-                        )
-                nc.scalar.copy(
-                    out=gr32[:, 2 * b : 2 * b + 2, :, :],
-                    in_=xt[:].rearrange("p (r u) m -> p r m u", u=2),
-                )
+        def quant_w(h):
             nc.vector.quantize_mx(
-                out=g_codes[:, j * QG * P : (j + 1) * QG * P].bitcast(E5M2X4),
-                scales=g_scales[:, j * QG * P : (j + 1) * QG * P],
-                in_=grouped[:],
+                out=w_codes[:, h * HALF : (h + 1) * HALF].bitcast(E4M3X4),
+                scales=w_scales[:, h * HALF : (h + 1) * HALF],
+                in_=w_grp[:, 4 * h * HALF : 4 * (h + 1) * HALF],
             )
 
+        banks = {}
+        grouped_of = {}
+
+        def transposes(b):
+            xt = psum_t.tile([P, 4, P], F32, name="xt")
+            banks[b] = xt
+            for rr in range(2):
+                g_sb, k = g_tiles[2 * b + rr]
+                words = g_sb[:].bitcast(F32)
+                for u in range(2):
+                    nc.tensor.transpose(
+                        xt[:, 2 * rr + u, :],
+                        words[:, k * 256 + 128 * u : k * 256 + 128 * u + 128],
+                        ident[:],
+                    )
+
+        def copy_out(b, eng):
+            grouped = stage.tile([P, 1024], BF16, name="grouped", align_bytes=64)
+            grouped_of[b] = grouped
+            gr32 = grouped[:].bitcast(F32).rearrange("p (r m u) -> p r m u", r=2, u=2)
+            src = banks[b][:].rearrange("p (r u) m -> p r m u", u=2)
+            if eng == "V":
+                nc.vector.tensor_copy(out=gr32, in_=src)
+            else:
+                nc.scalar.copy(out=gr32, in_=src)
+
+        def quant_g(b):
+            c0 = b * 2 * P
+            c1 = c0 + 2 * P
+            nc.vector.quantize_mx(
+                out=g_codes[:, c0:c1].bitcast(E5M2X4), scales=g_scales[:, c0:c1], in_=grouped_of[b][:]
+            )
+
+        accs = {}
+
+        def mx(r, h):
+            acc = psum_o.tile([P, HALF], F32, name="acc")
+            accs[(r, h)] = acc
+            nc.tensor.matmul_mx(
+                out=acc[:],
+                lhsT=g_codes[:, r * P : (r + 1) * P].bitcast(E5M2X4),
+                lhsT_scale=g_scales[:, r * P : (r + 1) * P],
+                rhs=w_codes[:, h * HALF : (h + 1) * HALF].bitcast(E4M3X4),
+                rhs_scale=w_scales[:, h * HALF : (h + 1) * HALF],
+                start=True,
+                stop=True,
+            )
+
+        def evac(dst, r, h, eng):
+            if eng == "V":
+                nc.vector.tensor_copy(out=dst, in_=accs[(r, h)][:])
+            else:
+                nc.scalar.copy(out=dst, in_=accs[(r, h)][:])
+
+        o_a0 = keep.tile([P, 2, HALF], F32, name="o_a0")
+        o_a1 = keep.tile([P, 2, HALF], F32, name="o_a1")
+        sign(0)
+        sign_on_vector(1)
+        sign(2)
+        transposes(0)
+        transposes(1)
+        copy_out(0, "S")
+        sign(3)
+        mul(0)
+        mul(1)
+        quant_w(0)
+        quant_g(0)
+        transposes(2)
+        mx(0, 0)
+        mx(1, 0)
+        mul(2)
+        mul(3)
+        quant_w(1)
+        evac(o_a0[:, 0, :], 0, 0, "S")
+        evac(o_a0[:, 1, :], 1, 0, "S")
+        nc.sync.dma_start(out=out_view[:, 0:2, 0:HALF], in_=o_a0[:])
+        copy_out(1, "S")
+        mx(0, 1)
+        mx(1, 1)
+        transposes(3)
+        quant_g(1)
+        evac(o_a1[:, 0, :], 0, 1, "S")
+        evac(o_a1[:, 1, :], 1, 1, "V")
+        nc.sync.dma_start(out=out_view[:, 0:2, HALF:IN_F], in_=o_a1[:])
+
         store_of = {}
-        r0 = 0
+        r0 = 2
         for si, n in enumerate(STORE_GROUPS):
             for k in range(n):
                 store_of[r0 + k] = (si, k, n, r0)
             r0 += n
+        assert r0 == NT
         o_tiles = {}
-
-        def multiply(r):
-            si, k, n, first = store_of[r]
-            if k == 0:
-                o_tiles[si] = keep.tile([P, n, IN_F], F32, name="o_sb%d" % si)
-            o_sb = o_tiles[si]
-            for h in range(2):
-                acc = psum_o.tile([P, HALF], F32, name="acc")
-                nc.tensor.matmul_mx(
-                    out=acc[:],
-                    lhsT=g_codes[:, r * P : (r + 1) * P].bitcast(E5M2X4),
-                    lhsT_scale=g_scales[:, r * P : (r + 1) * P],
-                    rhs=w_codes[:, h * HALF : (h + 1) * HALF].bitcast(E4M3X4),
-                    rhs_scale=w_scales[:, h * HALF : (h + 1) * HALF],
-                    start=True,
-                    stop=True,
-                )
-                if h == 0:
-                    nc.vector.tensor_copy(out=o_sb[:, k, 0:HALF], in_=acc[:])
-                else:
-                    nc.scalar.copy(out=o_sb[:, k, HALF:IN_F], in_=acc[:])
-            if k == n - 1:
-                nc.sync.dma_start(out=out_view[:, first : first + n, :], in_=o_sb[:])
-
-        n_q = NT // QG
-        prepare(0)
-        for j in range(n_q):
-            if j + 1 < n_q:
-                prepare(j + 1)
-            for r in range(j * QG, (j + 1) * QG):
-                multiply(r)
+        t_done = 4
+        copied = 2
+        prepared = 2
+        for b in range(1, NB):
+            for r in (2 * b, 2 * b + 1):
+                mx(r, 0)
+                mx(r, 1)
+            while t_done < NB and t_done < copied + 2:
+                transposes(t_done)
+                t_done += 1
+            for r in (2 * b, 2 * b + 1):
+                si, k, n, first = store_of[r]
+                if k == 0:
+                    o_tiles[si] = keep.tile([P, n, IN_F], F32, name="o_sb%d" % si)
+                o_sb = o_tiles[si]
+                evac(o_sb[:, k, 0:HALF], r, 0, "V")
+                evac(o_sb[:, k, HALF:IN_F], r, 1, "S")
+                if k == n - 1:
+                    nc.sync.dma_start(out=out_view[:, first : first + n, :], in_=o_sb[:])
+                if copied < t_done and copied <= b + LEAD:
+                    copy_out(copied, "S")
+                    copied += 1
+                if prepared < copied:
+                    quant_g(prepared)
+                    prepared += 1

@@ -16,19 +16,20 @@ P = 128
 TOKENS = 4096
 OUT_F = 512
 IN_F = 1024
-GROUPS = 8
+GROUP = 128
+GROUPS = IN_F // GROUP
 NT = TOKENS // P
+NB = NT // 2
 HALF = 512
+PIECE = 256
+PSUM_BANKS = 8
 
 FLOPS = 2 * TOKENS * OUT_F * IN_F
 BYTES = TOKENS * OUT_F * 2 + OUT_F * IN_F * 2 + OUT_F * GROUPS * 2 + TOKENS * IN_F * 4
 
-MANUAL = True
 LOAD_CHUNKS = [4, 4, 8, 8, 8]
-STORE_GROUPS = [1, 1, 1, 1, 1, 1, 1, 1, 2, 2, 2, 4, 4, 4, 4]
-LEAD = 2
-PC = 256
-NB = NT // 2
+HALF_TILES = 4
+STORE_GROUPS = [1, 1, 1, 1, 2, 2, 2, 2, 4, 4, 4, 4]
 
 
 def tile_stebitlinear_t_kernel(tc, x, sign_weights, scales, grad_out, out):
@@ -37,24 +38,27 @@ def tile_stebitlinear_t_kernel(tc, x, sign_weights, scales, grad_out, out):
     out_view = out.flatten_outer_dims().rearrange("(p r) i -> p r i", r=NT)
 
     with ExitStack() as ctx:
-        if MANUAL:
-            ctx.enter_context(tc.manual_schedule())
+        ctx.enter_context(tc.manual_schedule())
         keep = ctx.enter_context(tc.tile_pool(name="keep", bufs=1))
         stage = ctx.enter_context(tc.tile_pool(name="stage", bufs=4))
-        psum_t = ctx.enter_context(tc.psum_pool(name="psum_t", bufs=2))
-        psum_o = ctx.enter_context(tc.psum_pool(name="psum_o", bufs=6))
+        psum = ctx.enter_context(tc.psum_pool(name="psum", bufs=1))
 
         sc_raw = keep.tile([P, 4, GROUPS], BF16, name="sc_raw")
         nc.scalar.dma_start(
             out=sc_raw[:].rearrange("p (u e) g -> p u (e g)", u=2),
             in_=scales.rearrange("(u q s) -> q u s", u=2, s=2 * GROUPS),
         )
-        w_raw = keep.tile([P, 4, IN_F], BF16, name="w_raw")
-        for u in range(2):
-            nc.sync.dma_start(
-                out=w_raw[:, 2 * u : 2 * u + 2, :],
-                in_=sign_weights[256 * u : 256 * u + 256, :].rearrange("(q e) c -> q e c", e=2),
-            )
+        w_raw = []
+        for h in range(2):
+            raw = keep.tile([P, 4, HALF], BF16, name="w_raw%d" % h)
+            w_raw.append(raw)
+            for u in range(2):
+                nc.sync.dma_start(
+                    out=raw[:, 2 * u : 2 * u + 2, :],
+                    in_=sign_weights[256 * u : 256 * u + 256, h * HALF : (h + 1) * HALF].rearrange(
+                        "(q e) c -> q e c", e=2
+                    ),
+                )
         g_tiles = []
         r0 = 0
         for ci, n in enumerate(LOAD_CHUNKS):
@@ -83,51 +87,64 @@ def tile_stebitlinear_t_kernel(tc, x, sign_weights, scales, grad_out, out):
         g_codes = keep.tile([P, TOKENS], U32, name="g_codes", align_bytes=64)
         g_scales = keep.tile([P, TOKENS], U8, name="g_scales", align_bytes=64)
 
-        def sign(pc):
-            c0 = pc * PC
+        def raw_piece(pc):
+            c0 = (pc % 2) * PIECE
+            return w_raw[pc // 2][:, :, c0 : c0 + PIECE]
+
+        def grouped_piece(tile_, pc):
+            return tile_[:, 4 * pc * PIECE : 4 * (pc + 1) * PIECE]
+
+        def sign_on_scalar(pc):
             nc.scalar.activation(
-                out=sgn[:, 4 * c0 : 4 * (c0 + PC)].rearrange("p (c i t) -> p c t i", i=4, t=4),
-                in_=w_raw[:, :, c0 : c0 + PC].rearrange("p t (c i) -> p c t i", i=4),
+                out=grouped_piece(sgn, pc).rearrange("p (c i t) -> p c t i", i=4, t=4),
+                in_=raw_piece(pc).rearrange("p t (c i) -> p c t i", i=4),
                 func=ACT.Sign,
             )
 
         def sign_on_vector(pc):
-            c0 = pc * PC
             tiny = 2.0 ** -69
-            clipped = keep.tile([P, 4, PC], BF16, name="clipped")
+            clipped = keep.tile([P, 4, PIECE], BF16, name="clipped")
             nc.vector.tensor_scalar(
-                out=clipped[:], in0=w_raw[:, :, c0 : c0 + PC],
+                out=clipped[:], in0=raw_piece(pc),
                 scalar1=2.0 ** 64, scalar2=tiny, op0=ALU.mult, op1=ALU.min,
             )
             nc.vector.tensor_scalar(
-                out=sgn[:, 4 * c0 : 4 * (c0 + PC)].rearrange("p (c i t) -> p c t i", i=4, t=4),
+                out=grouped_piece(sgn, pc).rearrange("p (c i t) -> p c t i", i=4, t=4),
                 in0=clipped[:].rearrange("p t (c i) -> p c t i", i=4),
                 scalar1=-tiny, scalar2=2.0 ** 69, op0=ALU.max, op1=ALU.mult,
             )
 
-        def mul(pc):
-            c0 = pc * PC
-            ng = PC // 128
+        def scale_piece(pc):
+            ng = PIECE // GROUP
             nc.vector.tensor_tensor(
-                out=w_grp[:, 4 * c0 : 4 * (c0 + PC)].rearrange("p (g c t) -> p g c t", g=ng, t=4),
-                in0=sgn[:, 4 * c0 : 4 * (c0 + PC)].rearrange("p (g c t) -> p g c t", g=ng, t=4),
-                in1=sc_gt[:, pc * ng : (pc + 1) * ng, :].unsqueeze(2).to_broadcast([P, ng, 128, 4]),
+                out=grouped_piece(w_grp, pc).rearrange("p (g c t) -> p g c t", g=ng, t=4),
+                in0=grouped_piece(sgn, pc).rearrange("p (g c t) -> p g c t", g=ng, t=4),
+                in1=sc_gt[:, pc * ng : (pc + 1) * ng, :].unsqueeze(2).to_broadcast([P, ng, GROUP, 4]),
                 op=ALU.mult,
             )
 
-        def quant_w(h):
+        def quantise_weight(h):
             nc.vector.quantize_mx(
                 out=w_codes[:, h * HALF : (h + 1) * HALF].bitcast(E4M3X4),
                 scales=w_scales[:, h * HALF : (h + 1) * HALF],
                 in_=w_grp[:, 4 * h * HALF : 4 * (h + 1) * HALF],
             )
 
-        banks = {}
-        grouped_of = {}
+        free_banks = list(range(PSUM_BANKS))
+        taken = {"n": 0}
 
-        def transposes(b):
-            xt = psum_t.tile([P, 4, P], F32, name="xt")
-            banks[b] = xt
+        def take_bank(shape, name):
+            bank = free_banks[taken["n"]]
+            taken["n"] += 1
+            return psum.tile(shape, F32, name=name, tag="bank%d" % bank), bank
+
+        flipped = {}
+        grouped_of = {}
+        sums = {}
+
+        def transpose_pair(b):
+            xt, bank = take_bank([P, 4, P], "xt")
+            flipped[b] = (xt, bank)
             for rr in range(2):
                 g_sb, k = g_tiles[2 * b + rr]
                 words = g_sb[:].bitcast(F32)
@@ -138,28 +155,25 @@ def tile_stebitlinear_t_kernel(tc, x, sign_weights, scales, grad_out, out):
                         ident[:],
                     )
 
-        def copy_out(b, eng):
+        def copy_pair(b):
+            xt, bank = flipped[b]
             grouped = stage.tile([P, 1024], BF16, name="grouped", align_bytes=64)
             grouped_of[b] = grouped
-            gr32 = grouped[:].bitcast(F32).rearrange("p (r m u) -> p r m u", r=2, u=2)
-            src = banks[b][:].rearrange("p (r u) m -> p r m u", u=2)
-            if eng == "V":
-                nc.vector.tensor_copy(out=gr32, in_=src)
-            else:
-                nc.scalar.copy(out=gr32, in_=src)
+            nc.scalar.copy(
+                out=grouped[:].bitcast(F32).rearrange("p (r m u) -> p r m u", r=2, u=2),
+                in_=xt[:].rearrange("p (r u) m -> p r m u", u=2),
+            )
+            free_banks.append(bank)
 
-        def quant_g(b):
-            c0 = b * 2 * P
-            c1 = c0 + 2 * P
+        def quantise_pair(b):
+            cols = slice(b * 2 * P, (b + 1) * 2 * P)
             nc.vector.quantize_mx(
-                out=g_codes[:, c0:c1].bitcast(E5M2X4), scales=g_scales[:, c0:c1], in_=grouped_of[b][:]
+                out=g_codes[:, cols].bitcast(E5M2X4), scales=g_scales[:, cols], in_=grouped_of[b][:]
             )
 
-        accs = {}
-
-        def mx(r, h):
-            acc = psum_o.tile([P, HALF], F32, name="acc")
-            accs[(r, h)] = acc
+        def multiply(r, h):
+            acc, bank = take_bank([P, HALF], "acc")
+            sums[(r, h)] = (acc, bank)
             nc.tensor.matmul_mx(
                 out=acc[:],
                 lhsT=g_codes[:, r * P : (r + 1) * P].bitcast(E5M2X4),
@@ -170,73 +184,81 @@ def tile_stebitlinear_t_kernel(tc, x, sign_weights, scales, grad_out, out):
                 stop=True,
             )
 
-        def evac(dst, r, h, eng):
-            if eng == "V":
-                nc.vector.tensor_copy(out=dst, in_=accs[(r, h)][:])
+        def empty(dst, r, h, engine):
+            acc, bank = sums[(r, h)]
+            if engine == "vector":
+                nc.vector.tensor_copy(out=dst, in_=acc[:])
             else:
-                nc.scalar.copy(out=dst, in_=accs[(r, h)][:])
+                nc.scalar.copy(out=dst, in_=acc[:])
+            free_banks.append(bank)
 
-        o_a0 = keep.tile([P, 2, HALF], F32, name="o_a0")
-        o_a1 = keep.tile([P, 2, HALF], F32, name="o_a1")
-        sign(0)
+        sign_on_scalar(0)
         sign_on_vector(1)
-        sign(2)
-        transposes(0)
-        transposes(1)
-        copy_out(0, "S")
-        sign(3)
-        mul(0)
-        mul(1)
-        quant_w(0)
-        quant_g(0)
-        transposes(2)
-        mx(0, 0)
-        mx(1, 0)
-        mul(2)
-        mul(3)
-        quant_w(1)
-        evac(o_a0[:, 0, :], 0, 0, "S")
-        evac(o_a0[:, 1, :], 1, 0, "S")
-        nc.sync.dma_start(out=out_view[:, 0:2, 0:HALF], in_=o_a0[:])
-        copy_out(1, "S")
-        mx(0, 1)
-        mx(1, 1)
-        transposes(3)
-        quant_g(1)
-        evac(o_a1[:, 0, :], 0, 1, "S")
-        evac(o_a1[:, 1, :], 1, 1, "V")
-        nc.sync.dma_start(out=out_view[:, 0:2, HALF:IN_F], in_=o_a1[:])
+        sign_on_scalar(2)
+        for b in range(4):
+            transpose_pair(b)
+        scale_piece(0)
+        scale_piece(1)
+        quantise_weight(0)
+        copy_pair(0)
+        sign_on_scalar(3)
+        copy_pair(1)
+        quantise_pair(0)
+        multiply(0, 0)
+        multiply(1, 0)
+        scale_piece(2)
+        quantise_pair(1)
+        multiply(2, 0)
+        multiply(3, 0)
+        scale_piece(3)
+        quantise_weight(1)
+
+        def half_store(first, h, engines):
+            o_half = keep.tile([P, 2, HALF], F32, name="o_half%d_%d" % (first, h))
+            for k in range(2):
+                empty(o_half[:, k, :], first + k, h, engines[k])
+            nc.sync.dma_start(
+                out=out_view[:, first : first + 2, h * HALF : (h + 1) * HALF], in_=o_half[:]
+            )
+
+        half_store(0, 0, ("scalar", "scalar"))
+        half_store(2, 0, ("scalar", "vector"))
+        for r in range(HALF_TILES):
+            multiply(r, 1)
+        copy_pair(2)
+        half_store(0, 1, ("vector", "scalar"))
+        half_store(2, 1, ("vector", "scalar"))
+        quantise_pair(2)
+        copy_pair(3)
+        quantise_pair(3)
 
         store_of = {}
-        r0 = 2
+        r0 = HALF_TILES
         for si, n in enumerate(STORE_GROUPS):
             for k in range(n):
                 store_of[r0 + k] = (si, k, n, r0)
             r0 += n
         assert r0 == NT
         o_tiles = {}
-        t_done = 4
-        copied = 2
-        prepared = 2
-        for b in range(1, NB):
-            for r in (2 * b, 2 * b + 1):
-                mx(r, 0)
-                mx(r, 1)
-            while t_done < NB and t_done < copied + 2:
-                transposes(t_done)
-                t_done += 1
-            for r in (2 * b, 2 * b + 1):
-                si, k, n, first = store_of[r]
-                if k == 0:
-                    o_tiles[si] = keep.tile([P, n, IN_F], F32, name="o_sb%d" % si)
-                o_sb = o_tiles[si]
-                evac(o_sb[:, k, 0:HALF], r, 0, "V")
-                evac(o_sb[:, k, HALF:IN_F], r, 1, "S")
-                if k == n - 1:
-                    nc.sync.dma_start(out=out_view[:, first : first + n, :], in_=o_sb[:])
-                if copied < t_done and copied <= b + LEAD:
-                    copy_out(copied, "S")
-                    copied += 1
-                if prepared < copied:
-                    quant_g(prepared)
-                    prepared += 1
+        multiply(HALF_TILES, 0)
+        multiply(HALF_TILES, 1)
+        for r in range(HALF_TILES, NT):
+            if r + 1 < NT:
+                multiply(r + 1, 0)
+                multiply(r + 1, 1)
+            b = r // 2 + 2
+            if r % 2 == 0 and b < NB:
+                transpose_pair(b)
+            si, k, n, first = store_of[r]
+            if k == 0:
+                o_tiles[si] = keep.tile([P, n, IN_F], F32, name="o_sb%d" % si)
+            o_sb = o_tiles[si]
+            empty(o_sb[:, k, 0:HALF], r, 0, "vector")
+            empty(o_sb[:, k, HALF:IN_F], r, 1, "scalar")
+            if k == n - 1:
+                nc.sync.dma_start(out=out_view[:, first : first + n, :], in_=o_sb[:])
+            if b < NB:
+                if r % 2 == 0:
+                    copy_pair(b)
+                else:
+                    quantise_pair(b)

@@ -23,13 +23,14 @@ NB = NT // 2
 HALF = 512
 PIECE = 256
 PSUM_BANKS = 8
+REPEAT = 16
 
 FLOPS = 2 * TOKENS * OUT_F * IN_F
 BYTES = TOKENS * OUT_F * 2 + OUT_F * IN_F * 2 + OUT_F * GROUPS * 2 + TOKENS * IN_F * 4
 
-LOAD_CHUNKS = [4, 4, 8, 8, 8]
+LOAD_CHUNKS = [4, 4, 8, 16]
 HALF_TILES = 4
-STORE_GROUPS = [1, 1, 1, 1, 2, 2, 2, 2, 4, 4, 4, 4]
+STORE_GROUPS = [1, 1, 1, 1, 2, 2, 2, 2, 3, 3, 3, 3, 4]
 
 
 def tile_stebitlinear_t_kernel(tc, x, sign_weights, scales, grad_out, out):
@@ -78,8 +79,11 @@ def tile_stebitlinear_t_kernel(tc, x, sign_weights, scales, grad_out, out):
         nc.vector.memset(warm[:], 0.0)
         nc.scalar.activation(out=warm2[:], in_=warm[:], func=ACT.Sign)
 
-        sc_gt = keep.tile([P, GROUPS, 4], BF16, name="sc_gt")
-        nc.vector.tensor_copy(out=sc_gt[:], in_=sc_raw[:].rearrange("p t g -> p g t"))
+        sc_rep = keep.tile([P, GROUPS, REPEAT, 4], BF16, name="sc_rep")
+        nc.vector.tensor_copy(
+            out=sc_rep[:],
+            in_=sc_raw[:].rearrange("p t g -> p g t").unsqueeze(2).to_broadcast([P, GROUPS, REPEAT, 4]),
+        )
         sgn = keep.tile([P, IN_F * 4], BF16, name="sgn")
         w_grp = keep.tile([P, IN_F * 4], BF16, name="w_grp", align_bytes=64)
         w_codes = keep.tile([P, IN_F], U32, name="w_codes", align_bytes=64)
@@ -116,10 +120,14 @@ def tile_stebitlinear_t_kernel(tc, x, sign_weights, scales, grad_out, out):
 
         def scale_piece(pc):
             ng = PIECE // GROUP
+            run = 4 * REPEAT
             nc.vector.tensor_tensor(
-                out=grouped_piece(w_grp, pc).rearrange("p (g c t) -> p g c t", g=ng, t=4),
-                in0=grouped_piece(sgn, pc).rearrange("p (g c t) -> p g c t", g=ng, t=4),
-                in1=sc_gt[:, pc * ng : (pc + 1) * ng, :].unsqueeze(2).to_broadcast([P, ng, GROUP, 4]),
+                out=grouped_piece(w_grp, pc).rearrange("p (g a c) -> p g a c", g=ng, c=run),
+                in0=grouped_piece(sgn, pc).rearrange("p (g a c) -> p g a c", g=ng, c=run),
+                in1=sc_rep[:, pc * ng : (pc + 1) * ng, :, :]
+                .rearrange("p g c t -> p g (c t)")
+                .unsqueeze(2)
+                .to_broadcast([P, ng, GROUP // REPEAT, run]),
                 op=ALU.mult,
             )
 
@@ -159,10 +167,12 @@ def tile_stebitlinear_t_kernel(tc, x, sign_weights, scales, grad_out, out):
             xt, bank = flipped[b]
             grouped = stage.tile([P, 1024], BF16, name="grouped", align_bytes=64)
             grouped_of[b] = grouped
-            nc.scalar.copy(
-                out=grouped[:].bitcast(F32).rearrange("p (r m u) -> p r m u", r=2, u=2),
-                in_=xt[:].rearrange("p (r u) m -> p r m u", u=2),
-            )
+            dst = grouped[:].bitcast(F32).rearrange("p (r m u) -> p r m u", r=2, u=2)
+            src = xt[:].rearrange("p (r u) m -> p r m u", u=2)
+            if b % 4 == 3 and b > 3:
+                nc.vector.tensor_copy(out=dst, in_=src)
+            else:
+                nc.scalar.copy(out=dst, in_=src)
             free_banks.append(bank)
 
         def quantise_pair(b):

@@ -23,14 +23,13 @@ NB = NT // 2
 HALF = 512
 PIECE = 256
 PSUM_BANKS = 8
-REPEAT = 16
 
 FLOPS = 2 * TOKENS * OUT_F * IN_F
 BYTES = TOKENS * OUT_F * 2 + OUT_F * IN_F * 2 + OUT_F * GROUPS * 2 + TOKENS * IN_F * 4
 
-LOAD_CHUNKS = [4, 4, 8, 16]
+LOAD_CHUNKS = [4, 4, 8, 8, 8]
 HALF_TILES = 4
-STORE_GROUPS = [1, 1, 1, 1, 2, 2, 2, 2, 3, 3, 3, 3, 4]
+STORE_GROUPS = [1, 1, 1, 1, 2, 2, 2, 2, 4, 4, 4, 4]
 
 
 def tile_stebitlinear_t_kernel(tc, x, sign_weights, scales, grad_out, out):
@@ -49,17 +48,12 @@ def tile_stebitlinear_t_kernel(tc, x, sign_weights, scales, grad_out, out):
             out=sc_raw[:].rearrange("p (u e) g -> p u (e g)", u=2),
             in_=scales.rearrange("(u q s) -> q u s", u=2, s=2 * GROUPS),
         )
-        w_raw = []
-        for h in range(2):
-            raw = keep.tile([P, 4, HALF], BF16, name="w_raw%d" % h)
-            w_raw.append(raw)
-            for u in range(2):
-                nc.sync.dma_start(
-                    out=raw[:, 2 * u : 2 * u + 2, :],
-                    in_=sign_weights[256 * u : 256 * u + 256, h * HALF : (h + 1) * HALF].rearrange(
-                        "(q e) c -> q e c", e=2
-                    ),
-                )
+        w_raw = keep.tile([P, 4, IN_F], BF16, name="w_raw")
+        for u in range(2):
+            nc.sync.dma_start(
+                out=w_raw[:, 2 * u : 2 * u + 2, :],
+                in_=sign_weights[256 * u : 256 * u + 256, :].rearrange("(q e) c -> q e c", e=2),
+            )
         g_tiles = []
         r0 = 0
         for ci, n in enumerate(LOAD_CHUNKS):
@@ -79,11 +73,8 @@ def tile_stebitlinear_t_kernel(tc, x, sign_weights, scales, grad_out, out):
         nc.vector.memset(warm[:], 0.0)
         nc.scalar.activation(out=warm2[:], in_=warm[:], func=ACT.Sign)
 
-        sc_rep = keep.tile([P, GROUPS, REPEAT, 4], BF16, name="sc_rep")
-        nc.vector.tensor_copy(
-            out=sc_rep[:],
-            in_=sc_raw[:].rearrange("p t g -> p g t").unsqueeze(2).to_broadcast([P, GROUPS, REPEAT, 4]),
-        )
+        sc_gt = keep.tile([P, GROUPS, 4], BF16, name="sc_gt")
+        nc.vector.tensor_copy(out=sc_gt[:], in_=sc_raw[:].rearrange("p t g -> p g t"))
         sgn = keep.tile([P, IN_F * 4], BF16, name="sgn")
         w_grp = keep.tile([P, IN_F * 4], BF16, name="w_grp", align_bytes=64)
         w_codes = keep.tile([P, IN_F], U32, name="w_codes", align_bytes=64)
@@ -92,8 +83,7 @@ def tile_stebitlinear_t_kernel(tc, x, sign_weights, scales, grad_out, out):
         g_scales = keep.tile([P, TOKENS], U8, name="g_scales", align_bytes=64)
 
         def raw_piece(pc):
-            c0 = (pc % 2) * PIECE
-            return w_raw[pc // 2][:, :, c0 : c0 + PIECE]
+            return w_raw[:, :, pc * PIECE : (pc + 1) * PIECE]
 
         def grouped_piece(tile_, pc):
             return tile_[:, 4 * pc * PIECE : 4 * (pc + 1) * PIECE]
@@ -120,14 +110,10 @@ def tile_stebitlinear_t_kernel(tc, x, sign_weights, scales, grad_out, out):
 
         def scale_piece(pc):
             ng = PIECE // GROUP
-            run = 4 * REPEAT
             nc.vector.tensor_tensor(
-                out=grouped_piece(w_grp, pc).rearrange("p (g a c) -> p g a c", g=ng, c=run),
-                in0=grouped_piece(sgn, pc).rearrange("p (g a c) -> p g a c", g=ng, c=run),
-                in1=sc_rep[:, pc * ng : (pc + 1) * ng, :, :]
-                .rearrange("p g c t -> p g (c t)")
-                .unsqueeze(2)
-                .to_broadcast([P, ng, GROUP // REPEAT, run]),
+                out=grouped_piece(w_grp, pc).rearrange("p (g c t) -> p g c t", g=ng, t=4),
+                in0=grouped_piece(sgn, pc).rearrange("p (g c t) -> p g c t", g=ng, t=4),
+                in1=sc_gt[:, pc * ng : (pc + 1) * ng, :].unsqueeze(2).to_broadcast([P, ng, GROUP, 4]),
                 op=ALU.mult,
             )
 
@@ -167,12 +153,10 @@ def tile_stebitlinear_t_kernel(tc, x, sign_weights, scales, grad_out, out):
             xt, bank = flipped[b]
             grouped = stage.tile([P, 1024], BF16, name="grouped", align_bytes=64)
             grouped_of[b] = grouped
-            dst = grouped[:].bitcast(F32).rearrange("p (r m u) -> p r m u", r=2, u=2)
-            src = xt[:].rearrange("p (r u) m -> p r m u", u=2)
-            if b % 4 == 3 and b > 3:
-                nc.vector.tensor_copy(out=dst, in_=src)
-            else:
-                nc.scalar.copy(out=dst, in_=src)
+            nc.scalar.copy(
+                out=grouped[:].bitcast(F32).rearrange("p (r m u) -> p r m u", r=2, u=2),
+                in_=xt[:].rearrange("p (r u) m -> p r m u", u=2),
+            )
             free_banks.append(bank)
 
         def quantise_pair(b):

@@ -29,6 +29,7 @@ BYTES = TOKENS * OUT_F * 2 + OUT_F * IN_F * 2 + OUT_F * GROUPS * 2 + TOKENS * IN
 
 LOAD_CHUNKS = [4, 4, 8, 8, 8]
 HALF_TILES = 4
+RUN_PAIRS = 2
 STORE_GROUPS = [1, 1, 1, 1, 2, 2, 2, 2, 4, 4, 4, 4]
 
 
@@ -241,8 +242,9 @@ def tile_stebitlinear_t_kernel(tc, x, sign_weights, scales, grad_out, out):
                 multiply(r + 1, 0)
                 multiply(r + 1, 1)
             b = r // 2 + 2
-            if r % 2 == 0 and b < NB:
-                transpose_pair(b)
+            if r % (2 * RUN_PAIRS) == 0:
+                for bb in range(b, min(b + RUN_PAIRS, NB)):
+                    transpose_pair(bb)
             si, k, n, first = store_of[r]
             if k == 0:
                 o_tiles[si] = keep.tile([P, n, IN_F], F32, name="o_sb%d" % si)

@@ -23,6 +23,7 @@ NB = NT // 2
 HALF = 512
 PIECE = 256
 PSUM_BANKS = 8
+DMA_ALIGN = 256
 
 FLOPS = 2 * TOKENS * OUT_F * IN_F
 BYTES = TOKENS * OUT_F * 2 + OUT_F * IN_F * 2 + OUT_F * GROUPS * 2 + TOKENS * IN_F * 4
@@ -49,7 +50,7 @@ def tile_stebitlinear_t_kernel(tc, x, sign_weights, scales, grad_out, out):
             out=sc_raw[:].rearrange("p (u e) g -> p u (e g)", u=2),
             in_=scales.rearrange("(u q s) -> q u s", u=2, s=2 * GROUPS),
         )
-        w_raw = keep.tile([P, 4, IN_F], BF16, name="w_raw")
+        w_raw = keep.tile([P, 4, IN_F], BF16, name="w_raw", align_bytes=DMA_ALIGN)
         for u in range(2):
             nc.sync.dma_start(
                 out=w_raw[:, 2 * u : 2 * u + 2, :],
@@ -58,7 +59,7 @@ def tile_stebitlinear_t_kernel(tc, x, sign_weights, scales, grad_out, out):
         g_tiles = []
         r0 = 0
         for ci, n in enumerate(LOAD_CHUNKS):
-            g_sb = keep.tile([P, n * OUT_F], BF16, name="g_sb%d" % ci)
+            g_sb = keep.tile([P, n * OUT_F], BF16, name="g_sb%d" % ci, align_bytes=DMA_ALIGN)
             nc.sync.dma_start(
                 out=g_sb[:].rearrange("p (r o) -> p r o", r=n), in_=g_view[:, r0 : r0 + n, :]
             )
@@ -209,7 +210,9 @@ def tile_stebitlinear_t_kernel(tc, x, sign_weights, scales, grad_out, out):
         quantise_weight(1)
 
         def half_store(first, h, engines):
-            o_half = keep.tile([P, 2, HALF], F32, name="o_half%d_%d" % (first, h))
+            o_half = keep.tile(
+                [P, 2, HALF], F32, name="o_half%d_%d" % (first, h), align_bytes=DMA_ALIGN
+            )
             for k in range(2):
                 empty(o_half[:, k, :], first + k, h, engines[k])
             nc.sync.dma_start(
@@ -247,7 +250,9 @@ def tile_stebitlinear_t_kernel(tc, x, sign_weights, scales, grad_out, out):
                     transpose_pair(bb)
             si, k, n, first = store_of[r]
             if k == 0:
-                o_tiles[si] = keep.tile([P, n, IN_F], F32, name="o_sb%d" % si)
+                o_tiles[si] = keep.tile(
+                    [P, n, IN_F], F32, name="o_sb%d" % si, align_bytes=DMA_ALIGN
+                )
             o_sb = o_tiles[si]
             empty(o_sb[:, k, 0:HALF], r, 0, "vector")
             empty(o_sb[:, k, HALF:IN_F], r, 1, "scalar")

from contextlib import ExitStack

import concourse.mybir as mybir
from concourse.masks import make_identity

F32 = mybir.dt.float32
BF16 = mybir.dt.bfloat16
U32 = mybir.dt.uint32
U8 = mybir.dt.uint8
E4M3X4 = mybir.dt.float8_e4m3fn_x4
E5M2X4 = mybir.dt.float8_e5m2_x4
ACT = mybir.ActivationFunctionType
ALU = mybir.AluOpType

P = 128
TOKENS = 4096
OUT_F = 512
IN_F = 1024
GROUP = 128
GROUPS = IN_F // GROUP
NT = TOKENS // P
NB = NT // 2
HALF = 512
PIECE = 256
PSUM_BANKS = 8
DMA_ALIGN = 256

FLOPS = 2 * TOKENS * OUT_F * IN_F
BYTES = TOKENS * OUT_F * 2 + OUT_F * IN_F * 2 + OUT_F * GROUPS * 2 + TOKENS * IN_F * 4

LOAD_CHUNKS = [4, 4, 8, 8, 8]
HALF_TILES = 4
RUN_PAIRS = 2
STORE_GROUPS = [1, 1, 1, 1, 2, 2, 2, 2, 4, 4, 4, 4]


def tile_stebitlinear_t_kernel(tc, x, sign_weights, scales, grad_out, out):
    nc = tc.nc
    g_view = grad_out.flatten_outer_dims().rearrange("(p r) o -> p r o", r=NT)
    out_view = out.flatten_outer_dims().rearrange("(p r) i -> p r i", r=NT)

    with ExitStack() as ctx:
        ctx.enter_context(tc.manual_schedule())
        keep = ctx.enter_context(tc.tile_pool(name="keep", bufs=1))
        stage = ctx.enter_context(tc.tile_pool(name="stage", bufs=4))
        psum = ctx.enter_context(tc.psum_pool(name="psum", bufs=1))

        sc_raw = keep.tile([P, 4, GROUPS], BF16, name="sc_raw")
        nc.scalar.dma_start(
            out=sc_raw[:].rearrange("p (u e) g -> p u (e g)", u=2),
            in_=scales.rearrange("(u q s) -> q u s", u=2, s=2 * GROUPS),
        )
        w_raw = keep.tile([P, 4, IN_F], BF16, name="w_raw", align_bytes=DMA_ALIGN)
        for u in range(2):
            nc.sync.dma_start(
                out=w_raw[:, 2 * u : 2 * u + 2, :],
                in_=sign_weights[256 * u : 256 * u + 256, :].rearrange("(q e) c -> q e c", e=2),
            )
        g_tiles = []
        r0 = 0
        for ci, n in enumerate(LOAD_CHUNKS):
            g_sb = keep.tile([P, n * OUT_F], BF16, name="g_sb%d" % ci, align_bytes=DMA_ALIGN)
            nc.sync.dma_start(
                out=g_sb[:].rearrange("p (r o) -> p r o", r=n), in_=g_view[:, r0 : r0 + n, :]
            )
            for k in range(n):
                g_tiles.append((g_sb, k))
            r0 += n

        ident = keep.tile([P, P], F32, name="ident")
        make_identity(nc, ident[:])

        warm = keep.tile([P, 1], F32, name="warm")
        warm2 = keep.tile([P, 1], F32, name="warm2")
        nc.vector.memset(warm[:], 0.0)
        nc.scalar.activation(out=warm2[:], in_=warm[:], func=ACT.Sign)

        sc_gt = keep.tile([P, GROUPS, 4], BF16, name="sc_gt")
        nc.vector.tensor_copy(out=sc_gt[:], in_=sc_raw[:].rearrange("p t g -> p g t"))
        sgn = keep.tile([P, IN_F * 4], BF16, name="sgn")
        w_grp = keep.tile([P, IN_F * 4], BF16, name="w_grp", align_bytes=64)
        w_codes = keep.tile([P, IN_F], U32, name="w_codes", align_bytes=64)
        w_scales = keep.tile([P, IN_F], U8, name="w_scales", align_bytes=64)
        g_codes = keep.tile([P, TOKENS], U32, name="g_codes", align_bytes=64)
        g_scales = keep.tile([P, TOKENS], U8, name="g_scales", align_bytes=64)

        def raw_piece(pc):
            return w_raw[:, :, pc * PIECE : (pc + 1) * PIECE]

        def grouped_piece(tile_, pc):
            return tile_[:, 4 * pc * PIECE : 4 * (pc + 1) * PIECE]

        def sign_on_scalar(pc):
            nc.scalar.activation(
                out=grouped_piece(sgn, pc).rearrange("p (c i t) -> p c t i", i=4, t=4),
                in_=raw_piece(pc).rearrange("p t (c i) -> p c t i", i=4),
                func=ACT.Sign,
            )

        def sign_on_vector(pc):
            tiny = 2.0 ** -69
            clipped = keep.tile([P, 4, PIECE], BF16, name="clipped")
            nc.vector.tensor_scalar(
                out=clipped[:], in0=raw_piece(pc),
                scalar1=2.0 ** 64, scalar2=tiny, op0=ALU.mult, op1=ALU.min,
            )
            nc.vector.tensor_scalar(
                out=grouped_piece(sgn, pc).rearrange("p (c i t) -> p c t i", i=4, t=4),
                in0=clipped[:].rearrange("p t (c i) -> p c t i", i=4),
                scalar1=-tiny, scalar2=2.0 ** 69, op0=ALU.max, op1=ALU.mult,
            )

        def scale_piece(pc):
            ng = PIECE // GROUP
            nc.vector.tensor_tensor(
                out=grouped_piece(w_grp, pc).rearrange("p (g c t) -> p g c t", g=ng, t=4),
                in0=grouped_piece(sgn, pc).rearrange("p (g c t) -> p g c t", g=ng, t=4),
                in1=sc_gt[:, pc * ng : (pc + 1) * ng, :].unsqueeze(2).to_broadcast([P, ng, GROUP, 4]),
                op=ALU.mult,
            )

        def quantise_weight(h):
            nc.vector.quantize_mx(
                out=w_codes[:, h * HALF : (h + 1) * HALF].bitcast(E4M3X4),
                scales=w_scales[:, h * HALF : (h + 1) * HALF],
                in_=w_grp[:, 4 * h * HALF : 4 * (h + 1) * HALF],
            )

        free_banks = list(range(PSUM_BANKS))
        taken = {"n": 0}

        def take_bank(shape, name):
            bank = free_banks[taken["n"]]
            taken["n"] += 1
            return psum.tile(shape, F32, name=name, tag="bank%d" % bank), bank

        flipped = {}
        grouped_of = {}
        sums = {}

        def transpose_pair(b):
            xt, bank = take_bank([P, 4, P], "xt")
            flipped[b] = (xt, bank)
            for rr in range(2):
                g_sb, k = g_tiles[2 * b + rr]
                words = g_sb[:].bitcast(F32)
                for u in range(2):
                    nc.tensor.transpose(
                        xt[:, 2 * rr + u, :],
                        words[:, k * 256 + 128 * u : k * 256 + 128 * u + 128],
                        ident[:],
                    )

        def copy_pair(b):
            xt, bank = flipped[b]
            grouped = stage.tile([P, 1024], BF16, name="grouped", align_bytes=64)
            grouped_of[b] = grouped
            nc.scalar.copy(
                out=grouped[:].bitcast(F32).rearrange("p (r m u) -> p r m u", r=2, u=2),
                in_=xt[:].rearrange("p (r u) m -> p r m u", u=2),
            )
            free_banks.append(bank)

        def quantise_pair(b):
            cols = slice(b * 2 * P, (b + 1) * 2 * P)
            nc.vector.quantize_mx(
                out=g_codes[:, cols].bitcast(E5M2X4), scales=g_scales[:, cols], in_=grouped_of[b][:]
            )

        def multiply(r, h):
            acc, bank = take_bank([P, HALF], "acc")
            sums[(r, h)] = (acc, bank)
            nc.tensor.matmul_mx(
                out=acc[:],
                lhsT=g_codes[:, r * P : (r + 1) * P].bitcast(E5M2X4),
                lhsT_scale=g_scales[:, r * P : (r + 1) * P],
                rhs=w_codes[:, h * HALF : (h + 1) * HALF].bitcast(E4M3X4),
                rhs_scale=w_scales[:, h * HALF : (h + 1) * HALF],
                start=True,
                stop=True,
            )

        def empty(dst, r, h, engine):
            acc, bank = sums[(r, h)]
            if engine == "vector":
                nc.vector.tensor_copy(out=dst, in_=acc[:])
            else:
                nc.scalar.copy(out=dst, in_=acc[:])
            free_banks.append(bank)

        sign_on_scalar(0)
        sign_on_vector(1)
        sign_on_scalar(2)
        for b in range(4):
            transpose_pair(b)
        scale_piece(0)
        scale_piece(1)
        quantise_weight(0)
        copy_pair(0)
        sign_on_scalar(3)
        copy_pair(1)
        quantise_pair(0)
        multiply(0, 0)
        multiply(1, 0)
        scale_piece(2)
        quantise_pair(1)
        multiply(2, 0)
        multiply(3, 0)
        scale_piece(3)
        quantise_weight(1)

        def half_store(first, h, engines):
            o_half = keep.tile(
                [P, 2, HALF], F32, name="o_half%d_%d" % (first, h), align_bytes=DMA_ALIGN
            )
            for k in range(2):
                empty(o_half[:, k, :], first + k, h, engines[k])
            nc.sync.dma_start(
                out=out_view[:, first : first + 2, h * HALF : (h + 1) * HALF], in_=o_half[:]
            )

        half_store(0, 0, ("scalar", "scalar"))
        half_store(2, 0, ("scalar", "vector"))
        for r in range(HALF_TILES):
            multiply(r, 1)
        copy_pair(2)
        half_store(0, 1, ("vector", "scalar"))
        half_store(2, 1, ("vector", "scalar"))
        quantise_pair(2)
        copy_pair(3)
        quantise_pair(3)

        store_of = {}
        r0 = HALF_TILES
        for si, n in enumerate(STORE_GROUPS):
            for k in range(n):
                store_of[r0 + k] = (si, k, n, r0)
            r0 += n
        assert r0 == NT
        o_tiles = {}
        multiply(HALF_TILES, 0)
        multiply(HALF_TILES, 1)
        for r in range(HALF_TILES, NT):
            if r + 1 < NT:
                multiply(r + 1, 0)
                multiply(r + 1, 1)
            b = r // 2 + 2
            if r % (2 * RUN_PAIRS) == 0:
                for bb in range(b, min(b + RUN_PAIRS, NB)):
                    transpose_pair(bb)
            si, k, n, first = store_of[r]
            if k == 0:
                o_tiles[si] = keep.tile(
                    [P, n, IN_F], F32, name="o_sb%d" % si, align_bytes=DMA_ALIGN
                )
            o_sb = o_tiles[si]
            empty(o_sb[:, k, 0:HALF], r, 0, "vector")
            empty(o_sb[:, k, HALF:IN_F], r, 1, "scalar")
            if k == n - 1:
                nc.sync.dma_start(out=out_view[:, first : first + n, :], in_=o_sb[:])
            if b < NB:
                if r % 2 == 0:
                    copy_pair(b)
                else:
                    quantise_pair(b)
